import numpy as np
import ml_dtypes


def mxq(x, axis, fmt="e4m3"):
    dtype, down = {"e4m3": (ml_dtypes.float8_e4m3fn, 7), "e5m2": (ml_dtypes.float8_e5m2, 14)}[fmt]
    v = np.moveaxis(np.asarray(x, np.float32).astype(ml_dtypes.bfloat16).astype(np.float64), axis, -1)
    blocks = v.reshape(v.shape[:-1] + (-1, 32))
    amax = np.abs(blocks).max(-1, keepdims=True)
    byte = np.maximum(np.where(amax > 0, np.frexp(amax)[1] - 1 + 127, 0) - down, 1)
    scale = np.exp2(byte - 127.0)
    codes = (blocks / scale).astype(np.float32).astype(dtype).astype(np.float64)
    return np.moveaxis((codes * scale).reshape(v.shape), -1, axis)


WIDE = False


def mx_kscale(k):
    if not WIDE:
        return np.ones(k)
    levels = np.array([10, -10, 5, -5, 0])
    a = np.random.permutation(np.resize(levels, k // 512 * 4)).reshape(k // 512, 4)
    idx = np.arange(k)
    return np.exp2(a[idx // 512, idx % 128 // 32])


BF16 = ml_dtypes.bfloat16


def bf(x):
    return np.asarray(x, np.float32).astype(BF16)


def f64(x):
    return np.asarray(x).astype(np.float64)


B, CIN, COUT, T, R, C = 2, 1024, 128, 8, 16, 16


def setup_inputs():
    s = mx_kscale(CIN)
    x = np.random.standard_normal((B, CIN, T, R, C)) * s[None, :, None, None, None]
    W = np.random.standard_normal((7 * COUT, CIN)) * 0.5 / np.sqrt(CIN) / s[None, :]
    return {"x": bf(x), "W": bf(W)}


def _shift(a, axis, d):
    pads = [(0, 0)] * a.ndim
    idx = [slice(None)] * a.ndim
    if d > 0:
        pads[axis] = (1, 0)
        idx[axis] = slice(0, -1)
    else:
        pads[axis] = (0, 1)
        idx[axis] = slice(1, None)
    return np.pad(a, pads)[tuple(idx)]


def reference(x, W):
    cout = W.shape[0] // 7
    xq = mxq(f64(x), 1, "e4m3")
    Wq = mxq(f64(W), 1, "e4m3")
    all_out = xq.transpose(0, 2, 3, 4, 1) @ Wq.T
    a = all_out.reshape(*all_out.shape[:4], 7, cout)
    out = a[..., 0, :]
    out = out + _shift(a[..., 1, :], 1, +1)
    out = out + _shift(a[..., 2, :], 1, -1)
    out = out + _shift(a[..., 3, :], 2, +1)
    out = out + _shift(a[..., 4, :], 2, -1)
    out = out + _shift(a[..., 5, :], 3, +1)
    out = out + _shift(a[..., 6, :], 3, -1)
    return np.transpose(out, (0, 4, 1, 2, 3))

@@ -1,0 +1,201 @@
+from contextlib import ExitStack
+
+import concourse.mybir as mybir
+from concourse.masks import make_identity
+
+FLOPS = 2 * 4096 * 1024 * 896
+
+F32 = mybir.dt.float32
+BF16 = mybir.dt.bfloat16
+U32 = mybir.dt.uint32
+U8 = mybir.dt.uint8
+FP8X4 = mybir.dt.float8_e4m3fn_x4
+ADD = mybir.AluOpType.add
+
+P = 128
+PACK = 4
+G = 2
+SLICE = 256
+CHUNK = 512
+N_PAIRS = 8
+LINE = 16
+BASE = 16
+SPLIT = 320
+W_ORDER = (4, 0, 3, 1, 5, 6, 2)
+
+
+def tile_stackeddirectionalconv3d_t_kernel(tc, x, W, out):
+    nc = tc.nc
+    with ExitStack() as ctx:
+        keep = ctx.enter_context(tc.tile_pool(name="keep", bufs=1))
+        stage = ctx.enter_context(tc.tile_pool(name="stage", bufs=4))
+        psum = ctx.enter_context(tc.psum_pool(name="psum", bufs=4))
+
+        x_raw = keep.tile([P, N_PAIRS * G, PACK, CHUNK], BF16, name="x_raw")
+        x_codes = keep.tile([P, G, N_PAIRS * CHUNK], U32, name="x_codes", align_bytes=64)
+        x_scales = keep.tile([P, G, N_PAIRS * CHUNK], U8, name="x_scales", align_bytes=64)
+        w_codes = keep.tile([P, 7, G * P], U32, name="w_codes", align_bytes=64)
+        w_scales = keep.tile([P, 7, G * P], U8, name="w_scales", align_bytes=64)
+        zero_codes = keep.tile([P, P], U32, name="zero_codes", align_bytes=64)
+        zero_scales = keep.tile([P, P], U8, name="zero_scales", align_bytes=64)
+        ident = keep.tile([P, P], F32, name="ident")
+
+        zero_bf = keep.tile([P, P * PACK], BF16, name="zero_bf", align_bytes=64)
+        nc.vector.memset(zero_bf[:], 0.0)
+        nc.vector.quantize_mx(out=zero_codes[:].bitcast(FP8X4), scales=zero_scales[:], in_=zero_bf[:])
+        make_identity(nc, ident[:])
+
+        def load_x(q):
+            b, qq = divmod(q, 4)
+            xb = x[b].rearrange("k t r c -> k (t r c)")
+            for g in range(G):
+                rows = xb[512 * g : 512 * (g + 1), CHUNK * qq : CHUNK * (qq + 1)]
+                nc.sync.dma_start(
+                    out=x_raw[:, q * G + g, :, :],
+                    in_=rows.rearrange("(p j) w -> p j w", j=PACK),
+                )
+
+        w_raw = {}
+
+        def load_w(k):
+            w_raw[k] = keep.tile([P, 1024], BF16, name="w_raw%d" % k)
+            nc.sync.dma_start(out=w_raw[k][:], in_=W[P * k : P * (k + 1), :])
+
+        load_x(0)
+        for k in W_ORDER:
+            load_w(k)
+        for q in range(1, N_PAIRS):
+            load_x(q)
+
+        def prep_w(i, k):
+            words = w_raw[k][:].bitcast(F32).rearrange("o (g p u) -> o g u p", g=G, u=2)
+            wt = psum.tile([P, G, 2, P], F32, name="wt", tag="y")
+            for g in range(G):
+                for u in range(2):
+                    nc.tensor.transpose(wt[:, g, u, :], words[:, g, u, :], ident[:])
+            w_grouped = stage.tile([P, G * P * PACK], BF16, name="w_grouped", align_bytes=64)
+            dst = w_grouped[:].bitcast(F32).rearrange("p (g o u) -> p g o u", g=G, u=2)
+            src = wt[:].rearrange("p g u o -> p g o u")
+            if i % 2 == 0:
+                nc.vector.tensor_copy(out=dst, in_=src)
+            else:
+                nc.scalar.copy(out=dst, in_=src)
+            nc.vector.quantize_mx(
+                out=w_codes[:, k, :].bitcast(FP8X4), scales=w_scales[:, k, :], in_=w_grouped[:]
+            )
+
+        def prep_x(q):
+            tiles = []
+            for g in range(G):
+                grouped = stage.tile([P, CHUNK, PACK], BF16, name="grouped", align_bytes=64)
+                raw = x_raw[:, q * G + g, :, :]
+                nc.scalar.copy(
+                    out=grouped[:, 0:SPLIT, :].rearrange("p (c i) t -> p c t i", i=4),
+                    in_=raw[:, :, 0:SPLIT].rearrange("p t (c i) -> p c t i", i=4),
+                )
+                nc.vector.tensor_copy(
+                    out=grouped[:, SPLIT:CHUNK, :].rearrange("p (c i) t -> p c t i", i=4),
+                    in_=raw[:, :, SPLIT:CHUNK].rearrange("p t (c i) -> p c t i", i=4),
+                )
+                tiles.append(grouped)
+            for g in range(G):
+                cols = slice(CHUNK * q, CHUNK * (q + 1))
+                nc.vector.quantize_mx(
+                    out=x_codes[:, g, cols].bitcast(FP8X4),
+                    scales=x_scales[:, g, cols],
+                    in_=tiles[g][:].rearrange("p w j -> p (w j)"),
+                )
+
+        def passes(q):
+            main = [
+                psum.tile([P, 512], F32, name="main%d" % h, tag="m") for h in range(2)
+            ]
+            y5 = psum.tile([P, 512], F32, name="y5", tag="y")
+            y6 = psum.tile([P, 512], F32, name="y6", tag="y")
+            todo = []
+
+            def x_win(g, start, n):
+                return (
+                    x_codes[:, g, start : start + n].bitcast(FP8X4),
+                    x_scales[:, g, start : start + n],
+                )
+
+            def main_passes(k, shift, d):
+                for g in range(G):
+                    for h in range(2):
+                        s = 2 * q + h
+                        t = s % 8
+                        if t + d < 0 or t + d > 7:
+                            continue
+                        lo = BASE + shift
+                        todo.append(
+                            (h, main[h][:, lo : lo + SLICE], k, g, x_win(g, SLICE * (s + d), SLICE))
+                        )
+                    if k == 4 and g == 0:
+                        for h in range(2):
+                            todo.append(
+                                (
+                                    h,
+                                    main[h][:, SLICE : SLICE + P],
+                                    k,
+                                    g,
+                                    (zero_codes[:].bitcast(FP8X4), zero_scales[:]),
+                                )
+                            )
+
+            main_passes(4, -LINE, 0)
+            main_passes(0, 0, 0)
+            main_passes(3, LINE, 0)
+            main_passes(1, 0, -1)
+            for g in range(G):
+                todo.append((2, y5[:], 5, g, x_win(g, CHUNK * q, CHUNK)))
+            for g in range(G):
+                todo.append((3, y6[:], 6, g, x_win(g, CHUNK * q, CHUNK)))
+            main_passes(2, 0, 1)
+
+            first = {}
+            last = {}
+            for i, item in enumerate(todo):
+                if item[0] not in first:
+                    first[item[0]] = i
+                last[item[0]] = i
+            for i, (key, dst, k, g, rhs) in enumerate(todo):
+                nc.tensor.matmul_mx(
+                    out=dst,
+                    lhsT=w_codes[:, k, P * g : P * (g + 1)].bitcast(FP8X4),
+                    lhsT_scale=w_scales[:, k, P * g : P * (g + 1)],
+                    rhs=rhs[0],
+                    rhs_scale=rhs[1],
+                    start=(first[key] == i),
+                    stop=(last[key] == i),
+                )
+            return main, y5, y6
+
+        def finish(q, main, y5, y6):
+            b, qq = divmod(q, 4)
+            acc = stage.tile([P, CHUNK], F32, name="acc")
+            for h in range(2):
+                nc.scalar.copy(
+                    out=acc[:, SLICE * h : SLICE * (h + 1)], in_=main[h][:, BASE : BASE + SLICE]
+                )
+            acc3 = acc[:].rearrange("p (l c) -> p l c", c=LINE)
+            y53 = y5[:].rearrange("p (l c) -> p l c", c=LINE)
+            y63 = y6[:].rearrange("p (l c) -> p l c", c=LINE)
+            nc.vector.tensor_tensor(
+                out=acc3[:, :, 1:LINE], in0=acc3[:, :, 1:LINE], in1=y53[:, :, 0 : LINE - 1], op=ADD
+            )
+            nc.vector.tensor_tensor(
+                out=acc3[:, :, 0 : LINE - 1], in0=acc3[:, :, 0 : LINE - 1], in1=y63[:, :, 1:LINE], op=ADD
+            )
+            ob = out[b].rearrange("o t r c -> o (t r c)")
+            nc.sync.dma_start(out=ob[:, CHUNK * qq : CHUNK * (qq + 1)], in_=acc[:])
+
+        prep_x(0)
+        for i, k in enumerate(W_ORDER):
+            prep_w(i, k)
+        prep_x(1)
+        for q in range(N_PAIRS):
+            if q + 2 < N_PAIRS:
+                prep_x(q + 2)
+            main, y5, y6 = passes(q)
+            finish(q, main, y5, y6)

@@ -20,182 +20,243 @@ CHUNK = 512
 N_PAIRS = 8
 LINE = 16
 BASE = 16
+SPLIT_HEAD = 176
 SPLIT = 320
-W_ORDER = (4, 0, 3, 1, 5, 6, 2)
+W_ORDER = (6, 5, 4, 0, 3, 2, 1)
+PINNED = True
+HEAD_PAIRS = 2
+EARLY = 1
+HEAD_UNITS = [(0, 0, 0, SLICE), (0, 0, SLICE, SLICE), (0, 1, 0, SLICE), (0, 1, SLICE, SLICE)]
+UNITS = HEAD_UNITS + [(q, g, 0, CHUNK) for q in range(1, N_PAIRS) for g in range(G)]
 
 
 def tile_stackeddirectionalconv3d_t_kernel(tc, x, W, out):
     nc = tc.nc
     with ExitStack() as ctx:
+        if PINNED:
+            ctx.enter_context(tc.manual_schedule())
         keep = ctx.enter_context(tc.tile_pool(name="keep", bufs=1))
         stage = ctx.enter_context(tc.tile_pool(name="stage", bufs=4))
-        psum = ctx.enter_context(tc.psum_pool(name="psum", bufs=4))
+        psum = ctx.enter_context(tc.psum_pool(name="psum", bufs=1))
 
         x_raw = keep.tile([P, N_PAIRS * G, PACK, CHUNK], BF16, name="x_raw")
         x_codes = keep.tile([P, G, N_PAIRS * CHUNK], U32, name="x_codes", align_bytes=64)
         x_scales = keep.tile([P, G, N_PAIRS * CHUNK], U8, name="x_scales", align_bytes=64)
         w_codes = keep.tile([P, 7, G * P], U32, name="w_codes", align_bytes=64)
         w_scales = keep.tile([P, 7, G * P], U8, name="w_scales", align_bytes=64)
+        zero_bf = keep.tile([P, P * PACK], BF16, name="zero_bf", align_bytes=64)
         zero_codes = keep.tile([P, P], U32, name="zero_codes", align_bytes=64)
         zero_scales = keep.tile([P, P], U8, name="zero_scales", align_bytes=64)
         ident = keep.tile([P, P], F32, name="ident")
-
-        zero_bf = keep.tile([P, P * PACK], BF16, name="zero_bf", align_bytes=64)
-        nc.vector.memset(zero_bf[:], 0.0)
-        nc.vector.quantize_mx(out=zero_codes[:].bitcast(FP8X4), scales=zero_scales[:], in_=zero_bf[:])
-        make_identity(nc, ident[:])
-
-        def load_x(q):
-            b, qq = divmod(q, 4)
-            xb = x[b].rearrange("k t r c -> k (t r c)")
-            for g in range(G):
-                rows = xb[512 * g : 512 * (g + 1), CHUNK * qq : CHUNK * (qq + 1)]
-                nc.sync.dma_start(
-                    out=x_raw[:, q * G + g, :, :],
-                    in_=rows.rearrange("(p j) w -> p j w", j=PACK),
-                )
+        res = keep.tile([P, N_PAIRS, CHUNK], F32, name="res")
 
         w_raw = {}
-
-        def load_w(k):
+        for k in W_ORDER:
             w_raw[k] = keep.tile([P, 1024], BF16, name="w_raw%d" % k)
             nc.sync.dma_start(out=w_raw[k][:], in_=W[P * k : P * (k + 1), :])
+        for q, g, c0, n in UNITS:
+            b, qq = divmod(q, 4)
+            xb = x[b].rearrange("k t r c -> k (t r c)")
+            for u in range(2):
+                lo = 512 * g + 256 * u
+                rows = xb[lo : lo + 256, CHUNK * qq + c0 : CHUNK * qq + c0 + n]
+                nc.sync.dma_start(
+                    out=x_raw[:, q * G + g, 2 * u : 2 * u + 2, c0 : c0 + n],
+                    in_=rows.rearrange("(p e) w -> p e w", e=2),
+                )
 
-        load_x(0)
-        for k in W_ORDER:
-            load_w(k)
-        for q in range(1, N_PAIRS):
-            load_x(q)
+        make_identity(nc, ident[:])
+        nc.vector.memset(zero_bf[:], 0.0)
+        nc.vector.memset(
+            res[:].rearrange("p q (l c) -> p (q l) c", c=LINE)[:, :, LINE - 1 : LINE], 0.0
+        )
+        nc.vector.quantize_mx(out=zero_codes[:].bitcast(FP8X4), scales=zero_scales[:], in_=zero_bf[:])
 
-        def prep_w(i, k):
-            words = w_raw[k][:].bitcast(F32).rearrange("o (g p u) -> o g u p", g=G, u=2)
-            wt = psum.tile([P, G, 2, P], F32, name="wt", tag="y")
-            for g in range(G):
-                for u in range(2):
-                    nc.tensor.transpose(wt[:, g, u, :], words[:, g, u, :], ident[:])
-            w_grouped = stage.tile([P, G * P * PACK], BF16, name="w_grouped", align_bytes=64)
-            dst = w_grouped[:].bitcast(F32).rearrange("p (g o u) -> p g o u", g=G, u=2)
-            src = wt[:].rearrange("p g u o -> p g o u")
+        def bank(i, name):
+            return psum.tile([P, 512], F32, name=name, tag="bank%d" % i)
+
+        wt = {}
+        for i, k in enumerate(W_ORDER):
+            words = w_raw[k][:].bitcast(F32)
+            wt[k] = bank(i, "wt%d" % k)
+            for j in range(4):
+                nc.tensor.transpose(wt[k][:, P * j : P * (j + 1)], words[:, P * j : P * (j + 1)], ident[:])
+        w_grouped = {}
+
+        def w_copy(i, k):
+            w_grouped[k] = stage.tile([P, G * P * PACK], BF16, name="w_grouped", align_bytes=64)
+            dst = w_grouped[k][:].bitcast(F32).rearrange("p (g o u) -> p g o u", g=G, u=2)
+            src = wt[k][:].rearrange("p (g u o) -> p g o u", g=G, u=2)
             if i % 2 == 0:
-                nc.vector.tensor_copy(out=dst, in_=src)
-            else:
                 nc.scalar.copy(out=dst, in_=src)
+            else:
+                nc.vector.tensor_copy(out=dst, in_=src)
+
+        def w_quant(k):
             nc.vector.quantize_mx(
-                out=w_codes[:, k, :].bitcast(FP8X4), scales=w_scales[:, k, :], in_=w_grouped[:]
+                out=w_codes[:, k, :].bitcast(FP8X4), scales=w_scales[:, k, :], in_=w_grouped[k][:]
             )
 
-        def prep_x(q):
-            tiles = []
-            for g in range(G):
-                grouped = stage.tile([P, CHUNK, PACK], BF16, name="grouped", align_bytes=64)
-                raw = x_raw[:, q * G + g, :, :]
-                nc.scalar.copy(
-                    out=grouped[:, 0:SPLIT, :].rearrange("p (c i) t -> p c t i", i=4),
-                    in_=raw[:, :, 0:SPLIT].rearrange("p t (c i) -> p c t i", i=4),
-                )
-                nc.vector.tensor_copy(
-                    out=grouped[:, SPLIT:CHUNK, :].rearrange("p (c i) t -> p c t i", i=4),
-                    in_=raw[:, :, SPLIT:CHUNK].rearrange("p t (c i) -> p c t i", i=4),
-                )
-                tiles.append(grouped)
-            for g in range(G):
-                cols = slice(CHUNK * q, CHUNK * (q + 1))
-                nc.vector.quantize_mx(
-                    out=x_codes[:, g, cols].bitcast(FP8X4),
-                    scales=x_scales[:, g, cols],
-                    in_=tiles[g][:].rearrange("p w j -> p (w j)"),
-                )
+        for i, k in enumerate(W_ORDER):
+            w_copy(i, k)
+            if i >= 1:
+                w_quant(W_ORDER[i - 1])
+        w_quant(W_ORDER[6])
+
+        grouped = {}
+
+        def x_copy(unit):
+            q, g, c0, n = unit
+            split = (SPLIT_HEAD if q < HEAD_PAIRS else SPLIT) * n // CHUNK
+            t = stage.tile([P, CHUNK, PACK], BF16, name="grouped", align_bytes=64)
+            grouped[unit] = t
+            raw = x_raw[:, q * G + g, :, c0 : c0 + n]
+            nc.scalar.copy(
+                out=t[:, 0:split, :].rearrange("p (c i) t -> p c t i", i=4),
+                in_=raw[:, :, 0:split].rearrange("p t (c i) -> p c t i", i=4),
+            )
+            nc.vector.tensor_copy(
+                out=t[:, split:n, :].rearrange("p (c i) t -> p c t i", i=4),
+                in_=raw[:, :, split:n].rearrange("p t (c i) -> p c t i", i=4),
+            )
+
+        def x_quant(unit):
+            q, g, c0, n = unit
+            cols = slice(CHUNK * q + c0, CHUNK * q + c0 + n)
+            nc.vector.quantize_mx(
+                out=x_codes[:, g, cols].bitcast(FP8X4),
+                scales=x_scales[:, g, cols],
+                in_=grouped[unit][:, 0:n, :].rearrange("p w j -> p (w j)"),
+            )
+
+        SHIFT = {4: (-LINE, 0), 0: (0, 0), 3: (LINE, 0), 1: (0, -1), 2: (0, 1)}
+
+        def side(q, g, c0=0, n=CHUNK):
+            return [((q, 0), c0, n, 6, g, CHUNK * q + c0), ((q, 1), c0, n, 5, g, CHUNK * q + c0)]
+
+        def centre(q, h, g, ks):
+            s = 2 * q + h
+            found = []
+            for k in ks:
+                shift, d = SHIFT[k]
+                if not 0 <= s % 8 + d <= 7:
+                    continue
+                found.append(((q, 2 + h), BASE + shift, SLICE, k, g, SLICE * (s + d)))
+                if k == 4 and g == 0:
+                    found.append(((q, 2 + h), SLICE, P, k, g, None))
+            return found
+
+        def late(q, g):
+            return centre(q, 1, g, (2,)) if q >= 0 else []
+
+        plan = []
+        for q in range(N_PAIRS):
+            seg = []
+            if q == 0:
+                for g in range(G):
+                    seg += side(q, g, 0, SLICE) + centre(q, 0, g, (4, 0, 3))
+                    seg += side(q, g, SLICE, SLICE) + centre(q, 1, g, (4, 0, 3, 1)) + centre(q, 0, g, (2,))
+            elif q == 1:
+                for g in range(G):
+                    seg += late(q - 1, g) + side(q, g)
+                    seg += centre(q, 0, g, (4, 0, 3, 1, 2)) + centre(q, 1, g, (4, 0, 3, 1))
+            else:
+                for g in range(G):
+                    seg += late(q - 1, g)
+                for g in range(G):
+                    seg += side(q, g)
+                for h in range(2):
+                    for k in (4, 0, 3, 1, 2) if h == 0 else (4, 0, 3, 1):
+                        for g in range(G):
+                            seg += centre(q, h, g, (k,))
+            plan.append(seg)
+        flat = [item[0] for seg in plan for item in seg]
+        first = {}
+        last = {}
+        for i, key in enumerate(flat):
+            if key not in first:
+                first[key] = i
+            last[key] = i
+        banks = {}
+        count = [0]
 
         def passes(q):
-            main = [
-                psum.tile([P, 512], F32, name="main%d" % h, tag="m") for h in range(2)
-            ]
-            y5 = psum.tile([P, 512], F32, name="y5", tag="y")
-            y6 = psum.tile([P, 512], F32, name="y6", tag="y")
-            todo = []
-
-            def x_win(g, start, n):
-                return (
-                    x_codes[:, g, start : start + n].bitcast(FP8X4),
-                    x_scales[:, g, start : start + n],
-                )
-
-            def main_passes(k, shift, d):
-                for g in range(G):
-                    for h in range(2):
-                        s = 2 * q + h
-                        t = s % 8
-                        if t + d < 0 or t + d > 7:
-                            continue
-                        lo = BASE + shift
-                        todo.append(
-                            (h, main[h][:, lo : lo + SLICE], k, g, x_win(g, SLICE * (s + d), SLICE))
-                        )
-                    if k == 4 and g == 0:
-                        for h in range(2):
-                            todo.append(
-                                (
-                                    h,
-                                    main[h][:, SLICE : SLICE + P],
-                                    k,
-                                    g,
-                                    (zero_codes[:].bitcast(FP8X4), zero_scales[:]),
-                                )
-                            )
-
-            main_passes(4, -LINE, 0)
-            main_passes(0, 0, 0)
-            main_passes(3, LINE, 0)
-            main_passes(1, 0, -1)
-            for g in range(G):
-                todo.append((2, y5[:], 5, g, x_win(g, CHUNK * q, CHUNK)))
-            for g in range(G):
-                todo.append((3, y6[:], 6, g, x_win(g, CHUNK * q, CHUNK)))
-            main_passes(2, 0, 1)
-
-            first = {}
-            last = {}
-            for i, item in enumerate(todo):
-                if item[0] not in first:
-                    first[item[0]] = i
-                last[item[0]] = i
-            for i, (key, dst, k, g, rhs) in enumerate(todo):
+            for key, lo, n, k, g, xcol in plan[q]:
+                if key not in banks:
+                    banks[key] = bank(4 * (key[0] % 2) + key[1], "acc%d" % key[1])
+                if xcol is None:
+                    rhs, rhs_scale = zero_codes[:], zero_scales[:]
+                else:
+                    rhs, rhs_scale = x_codes[:, g, xcol : xcol + n], x_scales[:, g, xcol : xcol + n]
+                i = count[0]
+                count[0] = i + 1
                 nc.tensor.matmul_mx(
-                    out=dst,
+                    out=banks[key][:, lo : lo + n],
                     lhsT=w_codes[:, k, P * g : P * (g + 1)].bitcast(FP8X4),
                     lhsT_scale=w_scales[:, k, P * g : P * (g + 1)],
-                    rhs=rhs[0],
-                    rhs_scale=rhs[1],
+                    rhs=rhs.bitcast(FP8X4),
+                    rhs_scale=rhs_scale,
                     start=(first[key] == i),
                     stop=(last[key] == i),
                 )
-            return main, y5, y6
 
-        def finish(q, main, y5, y6):
+        def lines(ap):
+            return ap.rearrange("p (l c) -> p l c", c=LINE)
+
+        def side_copy(q):
+            nc.scalar.copy(
+                out=lines(res[:, q, :])[:, :, 0 : LINE - 1], in_=lines(banks[(q, 0)][:])[:, :, 1:LINE]
+            )
+
+        def side_add(q):
+            r3 = lines(res[:, q, :])
+            nc.vector.tensor_tensor(
+                out=r3[:, :, 1:LINE],
+                in0=r3[:, :, 1:LINE],
+                in1=lines(banks[(q, 1)][:])[:, :, 0 : LINE - 1],
+                op=ADD,
+            )
+
+        def finish(q, h):
+            cols = slice(SLICE * h, SLICE * (h + 1))
+            nc.vector.tensor_tensor(
+                out=res[:, q, cols],
+                in0=res[:, q, cols],
+                in1=banks[(q, 2 + h)][:, BASE : BASE + SLICE],
+                op=ADD,
+            )
+
+        def store(q, lo, n):
             b, qq = divmod(q, 4)
-            acc = stage.tile([P, CHUNK], F32, name="acc")
-            for h in range(2):
-                nc.scalar.copy(
-                    out=acc[:, SLICE * h : SLICE * (h + 1)], in_=main[h][:, BASE : BASE + SLICE]
-                )
-            acc3 = acc[:].rearrange("p (l c) -> p l c", c=LINE)
-            y53 = y5[:].rearrange("p (l c) -> p l c", c=LINE)
-            y63 = y6[:].rearrange("p (l c) -> p l c", c=LINE)
-            nc.vector.tensor_tensor(
-                out=acc3[:, :, 1:LINE], in0=acc3[:, :, 1:LINE], in1=y53[:, :, 0 : LINE - 1], op=ADD
-            )
-            nc.vector.tensor_tensor(
-                out=acc3[:, :, 0 : LINE - 1], in0=acc3[:, :, 0 : LINE - 1], in1=y63[:, :, 1:LINE], op=ADD
-            )
             ob = out[b].rearrange("o t r c -> o (t r c)")
-            nc.sync.dma_start(out=ob[:, CHUNK * qq : CHUNK * (qq + 1)], in_=acc[:])
+            nc.sync.dma_start(out=ob[:, CHUNK * qq + lo : CHUNK * qq + lo + n], in_=res[:, q, lo : lo + n])
 
-        prep_x(0)
-        for i, k in enumerate(W_ORDER):
-            prep_w(i, k)
-        prep_x(1)
+        for unit in HEAD_UNITS + [(1, 0, 0, CHUNK), (1, 1, 0, CHUNK)]:
+            x_copy(unit)
+            x_quant(unit)
         for q in range(N_PAIRS):
-            if q + 2 < N_PAIRS:
-                prep_x(q + 2)
-            main, y5, y6 = passes(q)
-            finish(q, main, y5, y6)
+            passes(q)
+            nxt = q + 2
+            if q >= 1:
+                finish(q - 1, 1)
+                store(q - 1, 0, CHUNK)
+            side_copy(q)
+            if q < EARLY:
+                side_add(q)
+                finish(q, 0)
+                for g in range(G):
+                    x_copy((nxt, g, 0, CHUNK))
+                    x_quant((nxt, g, 0, CHUNK))
+                continue
+            if nxt < N_PAIRS:
+                x_copy((nxt, 0, 0, CHUNK))
+                x_copy((nxt, 1, 0, CHUNK))
+            side_add(q)
+            if nxt < N_PAIRS:
+                x_quant((nxt, 0, 0, CHUNK))
+            finish(q, 0)
+            if nxt < N_PAIRS:
+                x_quant((nxt, 1, 0, CHUNK))
+        store(N_PAIRS - 1, 0, SLICE)
+        finish(N_PAIRS - 1, 1)
+        store(N_PAIRS - 1, SLICE, SLICE)

@@ -22,12 +22,16 @@ LINE = 16
 BASE = 16
 SPLIT_HEAD = 176
 SPLIT = 320
-W_ORDER = (6, 5, 4, 0, 3, 2, 1)
+W_FIRST = (6, 5, 4, 0, 3)
+W_LATER = (2, 1)
 PINNED = True
-HEAD_PAIRS = 2
+HEAD_PAIRS = 3
+FINE_PAIRS = 3
 EARLY = 1
-HEAD_UNITS = [(0, 0, 0, SLICE), (0, 0, SLICE, SLICE), (0, 1, 0, SLICE), (0, 1, SLICE, SLICE)]
-UNITS = HEAD_UNITS + [(q, g, 0, CHUNK) for q in range(1, N_PAIRS) for g in range(G)]
+W_ON_VECTOR = 0
+HEAD_UNITS = [(0, 0, 0, SLICE), (0, 0, SLICE, SLICE), (0, 1, 0, CHUNK)]
+UNITS = [(q, g, 0, CHUNK) for q in range(1, N_PAIRS) for g in range(G)]
+SPLIT_TRANSPOSES = False
 
 
 def tile_stackeddirectionalconv3d_t_kernel(tc, x, W, out):
@@ -36,12 +40,11 @@ def tile_stackeddirectionalconv3d_t_kernel(tc, x, W, out):
         if PINNED:
             ctx.enter_context(tc.manual_schedule())
         keep = ctx.enter_context(tc.tile_pool(name="keep", bufs=1))
-        stage = ctx.enter_context(tc.tile_pool(name="stage", bufs=4))
+        stage = ctx.enter_context(tc.tile_pool(name="stage", bufs=3))
         psum = ctx.enter_context(tc.psum_pool(name="psum", bufs=1))
 
-        x_raw = keep.tile([P, N_PAIRS * G, PACK, CHUNK], BF16, name="x_raw")
-        x_codes = keep.tile([P, G, N_PAIRS * CHUNK], U32, name="x_codes", align_bytes=64)
-        x_scales = keep.tile([P, G, N_PAIRS * CHUNK], U8, name="x_scales", align_bytes=64)
+        x_codes = keep.tile([P, N_PAIRS, G, CHUNK], U32, name="x_codes", align_bytes=64)
+        x_scales = keep.tile([P, N_PAIRS, G, CHUNK], U8, name="x_scales", align_bytes=64)
         w_codes = keep.tile([P, 7, G * P], U32, name="w_codes", align_bytes=64)
         w_scales = keep.tile([P, 7, G * P], U8, name="w_scales", align_bytes=64)
         zero_bf = keep.tile([P, P * PACK], BF16, name="zero_bf", align_bytes=64)
@@ -51,88 +54,127 @@ def tile_stackeddirectionalconv3d_t_kernel(tc, x, W, out):
         res = keep.tile([P, N_PAIRS, CHUNK], F32, name="res")
 
         w_raw = {}
-        for k in W_ORDER:
+
+        def load_w(k):
             w_raw[k] = keep.tile([P, 1024], BF16, name="w_raw%d" % k)
             nc.sync.dma_start(out=w_raw[k][:], in_=W[P * k : P * (k + 1), :])
-        for q, g, c0, n in UNITS:
+
+        x_raw = {}
+
+        def load_x(unit):
+            q, g, c0, n = unit
+            if q < FINE_PAIRS:
+                x_raw[unit] = keep.tile([P, PACK, n], BF16, name="x_raw_%d_%d_%d" % (q, g, c0))[:]
+            else:
+                if g == 0:
+                    x_raw[q] = keep.tile([P, G, PACK, CHUNK], BF16, name="x_raw_%d" % q)
+                x_raw[unit] = x_raw[q][:, g, :, :]
             b, qq = divmod(q, 4)
             xb = x[b].rearrange("k t r c -> k (t r c)")
             for u in range(2):
                 lo = 512 * g + 256 * u
                 rows = xb[lo : lo + 256, CHUNK * qq + c0 : CHUNK * qq + c0 + n]
                 nc.sync.dma_start(
-                    out=x_raw[:, q * G + g, 2 * u : 2 * u + 2, c0 : c0 + n],
+                    out=x_raw[unit][:, 2 * u : 2 * u + 2, :],
                     in_=rows.rearrange("(p e) w -> p e w", e=2),
                 )
 
+        for k in W_FIRST:
+            load_w(k)
+        load_x(HEAD_UNITS[0])
+        for k in W_LATER:
+            load_w(k)
+        for unit in HEAD_UNITS[1:] + UNITS:
+            load_x(unit)
+
+        def lines(ap):
+            return ap.rearrange("p (l c) -> p l c", c=LINE)
+
         make_identity(nc, ident[:])
         nc.vector.memset(zero_bf[:], 0.0)
-        nc.vector.memset(
-            res[:].rearrange("p q (l c) -> p (q l) c", c=LINE)[:, :, LINE - 1 : LINE], 0.0
-        )
+        nc.vector.memset(lines(res[:, N_PAIRS - 1, :])[:, :, LINE - 1 : LINE], 0.0)
         nc.vector.quantize_mx(out=zero_codes[:].bitcast(FP8X4), scales=zero_scales[:], in_=zero_bf[:])
 
         def bank(i, name):
             return psum.tile([P, 512], F32, name=name, tag="bank%d" % i)
 
         wt = {}
-        for i, k in enumerate(W_ORDER):
+
+        def w_transposes(i, k):
             words = w_raw[k][:].bitcast(F32)
             wt[k] = bank(i, "wt%d" % k)
             for j in range(4):
                 nc.tensor.transpose(wt[k][:, P * j : P * (j + 1)], words[:, P * j : P * (j + 1)], ident[:])
+
         w_grouped = {}
 
         def w_copy(i, k):
             w_grouped[k] = stage.tile([P, G * P * PACK], BF16, name="w_grouped", align_bytes=64)
             dst = w_grouped[k][:].bitcast(F32).rearrange("p (g o u) -> p g o u", g=G, u=2)
             src = wt[k][:].rearrange("p (g u o) -> p g o u", g=G, u=2)
-            if i % 2 == 0:
-                nc.scalar.copy(out=dst, in_=src)
-            else:
+            if W_ON_VECTOR and i % W_ON_VECTOR == W_ON_VECTOR - 1:
                 nc.vector.tensor_copy(out=dst, in_=src)
+            else:
+                nc.scalar.copy(out=dst, in_=src)
 
         def w_quant(k):
             nc.vector.quantize_mx(
                 out=w_codes[:, k, :].bitcast(FP8X4), scales=w_scales[:, k, :], in_=w_grouped[k][:]
             )
 
-        for i, k in enumerate(W_ORDER):
-            w_copy(i, k)
-            if i >= 1:
-                w_quant(W_ORDER[i - 1])
-        w_quant(W_ORDER[6])
-
         grouped = {}
+
+        def runs4(ap, order):
+            return ap.rearrange(order, i=4)
 
         def x_copy(unit):
             q, g, c0, n = unit
             split = (SPLIT_HEAD if q < HEAD_PAIRS else SPLIT) * n // CHUNK
             t = stage.tile([P, CHUNK, PACK], BF16, name="grouped", align_bytes=64)
             grouped[unit] = t
-            raw = x_raw[:, q * G + g, :, c0 : c0 + n]
+            raw = x_raw[unit]
             nc.scalar.copy(
-                out=t[:, 0:split, :].rearrange("p (c i) t -> p c t i", i=4),
-                in_=raw[:, :, 0:split].rearrange("p t (c i) -> p c t i", i=4),
+                out=runs4(t[:, 0:split, :], "p (c i) t -> p c t i"),
+                in_=runs4(raw[:, :, 0:split], "p t (c i) -> p c t i"),
             )
             nc.vector.tensor_copy(
-                out=t[:, split:n, :].rearrange("p (c i) t -> p c t i", i=4),
-                in_=raw[:, :, split:n].rearrange("p t (c i) -> p c t i", i=4),
+                out=runs4(t[:, split:n, :], "p (c i) t -> p c t i"),
+                in_=runs4(raw[:, :, split:n], "p t (c i) -> p c t i"),
             )
 
         def x_quant(unit):
             q, g, c0, n = unit
-            cols = slice(CHUNK * q + c0, CHUNK * q + c0 + n)
             nc.vector.quantize_mx(
-                out=x_codes[:, g, cols].bitcast(FP8X4),
-                scales=x_scales[:, g, cols],
+                out=x_codes[:, q, g, c0 : c0 + n].bitcast(FP8X4),
+                scales=x_scales[:, q, g, c0 : c0 + n],
                 in_=grouped[unit][:, 0:n, :].rearrange("p w j -> p (w j)"),
+            )
+
+        def pair_copy(q):
+            t = stage.tile([P, G, CHUNK, PACK], BF16, name="grouped2", align_bytes=64)
+            grouped[q] = t
+            raw = x_raw[q][:]
+            for g in range(G):
+                nc.scalar.copy(
+                    out=runs4(t[:, g, 0:SPLIT, :], "p (c i) t -> p c t i"),
+                    in_=runs4(raw[:, g, :, 0:SPLIT], "p t (c i) -> p c t i"),
+                )
+            nc.vector.tensor_copy(
+                out=runs4(t[:, :, SPLIT:CHUNK, :], "p g (c i) t -> p g c t i"),
+                in_=runs4(raw[:, :, :, SPLIT:CHUNK], "p g t (c i) -> p g c t i"),
+            )
+
+        def pair_quant(q):
+            nc.vector.quantize_mx(
+                out=x_codes[:, q, :, :].rearrange("p g c -> p (g c)").bitcast(FP8X4),
+                scales=x_scales[:, q, :, :].rearrange("p g c -> p (g c)"),
+                in_=grouped[q][:].rearrange("p g w j -> p (g w j)"),
             )
 
         SHIFT = {4: (-LINE, 0), 0: (0, 0), 3: (LINE, 0), 1: (0, -1), 2: (0, 1)}
 
         def side(q, g, c0=0, n=CHUNK):
-            return [((q, 0), c0, n, 6, g, CHUNK * q + c0), ((q, 1), c0, n, 5, g, CHUNK * q + c0)]
+            return [((q, 0), c0, n, 6, g, (q, c0)), ((q, 1), c0, n, 5, g, (q, c0))]
 
         def centre(q, h, g, ks):
             s = 2 * q + h
@@ -141,28 +183,25 @@ def tile_stackeddirectionalconv3d_t_kernel(tc, x, W, out):
                 shift, d = SHIFT[k]
                 if not 0 <= s % 8 + d <= 7:
                     continue
-                found.append(((q, 2 + h), BASE + shift, SLICE, k, g, SLICE * (s + d)))
+                found.append(((q, 2 + h), BASE + shift, SLICE, k, g, ((s + d) // 2, SLICE * ((s + d) % 2))))
                 if k == 4 and g == 0:
                     found.append(((q, 2 + h), SLICE, P, k, g, None))
             return found
-
-        def late(q, g):
-            return centre(q, 1, g, (2,)) if q >= 0 else []
 
         plan = []
         for q in range(N_PAIRS):
             seg = []
             if q == 0:
-                for g in range(G):
-                    seg += side(q, g, 0, SLICE) + centre(q, 0, g, (4, 0, 3))
-                    seg += side(q, g, SLICE, SLICE) + centre(q, 1, g, (4, 0, 3, 1)) + centre(q, 0, g, (2,))
+                plan.append(side(q, 0, 0, SLICE) + centre(q, 0, 0, (4, 0, 3)))
+                plan.append(side(q, 0, SLICE, SLICE) + centre(q, 1, 0, (4, 0, 3, 1)) + centre(q, 0, 0, (2,)))
+                seg += side(q, 1) + centre(q, 0, 1, (4, 0, 3, 2)) + centre(q, 1, 1, (4, 0, 3, 1))
             elif q == 1:
                 for g in range(G):
-                    seg += late(q - 1, g) + side(q, g)
+                    seg += centre(q - 1, 1, g, (2,)) + side(q, g)
                     seg += centre(q, 0, g, (4, 0, 3, 1, 2)) + centre(q, 1, g, (4, 0, 3, 1))
             else:
                 for g in range(G):
-                    seg += late(q - 1, g)
+                    seg += centre(q - 1, 1, g, (2,))
                 for g in range(G):
                     seg += side(q, g)
                 for h in range(2):
@@ -180,14 +219,15 @@ def tile_stackeddirectionalconv3d_t_kernel(tc, x, W, out):
         banks = {}
         count = [0]
 
-        def passes(q):
-            for key, lo, n, k, g, xcol in plan[q]:
+        def passes(part):
+            for key, lo, n, k, g, xat in plan[part]:
                 if key not in banks:
                     banks[key] = bank(4 * (key[0] % 2) + key[1], "acc%d" % key[1])
-                if xcol is None:
+                if xat is None:
                     rhs, rhs_scale = zero_codes[:], zero_scales[:]
                 else:
-                    rhs, rhs_scale = x_codes[:, g, xcol : xcol + n], x_scales[:, g, xcol : xcol + n]
+                    rhs = x_codes[:, xat[0], g, xat[1] : xat[1] + n]
+                    rhs_scale = x_scales[:, xat[0], g, xat[1] : xat[1] + n]
                 i = count[0]
                 count[0] = i + 1
                 nc.tensor.matmul_mx(
@@ -200,63 +240,91 @@ def tile_stackeddirectionalconv3d_t_kernel(tc, x, W, out):
                     stop=(last[key] == i),
                 )
 
-        def lines(ap):
-            return ap.rearrange("p (l c) -> p l c", c=LINE)
+        def main_copy(q, h):
+            nc.scalar.copy(
+                out=res[:, q, SLICE * h : SLICE * (h + 1)], in_=banks[(q, 2 + h)][:, BASE : BASE + SLICE]
+            )
+
+        def main_add(q, h):
+            cols = slice(SLICE * h, SLICE * (h + 1))
+            nc.vector.tensor_tensor(
+                out=res[:, q, cols], in0=res[:, q, cols], in1=banks[(q, 2 + h)][:, BASE : BASE + SLICE], op=ADD
+            )
 
         def side_copy(q):
             nc.scalar.copy(
                 out=lines(res[:, q, :])[:, :, 0 : LINE - 1], in_=lines(banks[(q, 0)][:])[:, :, 1:LINE]
             )
 
-        def side_add(q):
+        def side_add(q, which):
             r3 = lines(res[:, q, :])
-            nc.vector.tensor_tensor(
-                out=r3[:, :, 1:LINE],
-                in0=r3[:, :, 1:LINE],
-                in1=lines(banks[(q, 1)][:])[:, :, 0 : LINE - 1],
-                op=ADD,
-            )
-
-        def finish(q, h):
-            cols = slice(SLICE * h, SLICE * (h + 1))
-            nc.vector.tensor_tensor(
-                out=res[:, q, cols],
-                in0=res[:, q, cols],
-                in1=banks[(q, 2 + h)][:, BASE : BASE + SLICE],
-                op=ADD,
-            )
+            y3 = lines(banks[(q, which)][:])
+            if which == 1:
+                dst, src = r3[:, :, 1:LINE], y3[:, :, 0 : LINE - 1]
+            else:
+                dst, src = r3[:, :, 0 : LINE - 1], y3[:, :, 1:LINE]
+            nc.vector.tensor_tensor(out=dst, in0=dst, in1=src, op=ADD)
 
         def store(q, lo, n):
             b, qq = divmod(q, 4)
             ob = out[b].rearrange("o t r c -> o (t r c)")
             nc.sync.dma_start(out=ob[:, CHUNK * qq + lo : CHUNK * qq + lo + n], in_=res[:, q, lo : lo + n])
 
-        for unit in HEAD_UNITS + [(1, 0, 0, CHUNK), (1, 1, 0, CHUNK)]:
-            x_copy(unit)
-            x_quant(unit)
-        for q in range(N_PAIRS):
-            passes(q)
-            nxt = q + 2
-            if q >= 1:
-                finish(q - 1, 1)
-                store(q - 1, 0, CHUNK)
-            side_copy(q)
-            if q < EARLY:
-                side_add(q)
-                finish(q, 0)
+        def prepare(q):
+            if q >= N_PAIRS:
+                return
+            if q < FINE_PAIRS:
                 for g in range(G):
-                    x_copy((nxt, g, 0, CHUNK))
-                    x_quant((nxt, g, 0, CHUNK))
-                continue
-            if nxt < N_PAIRS:
-                x_copy((nxt, 0, 0, CHUNK))
-                x_copy((nxt, 1, 0, CHUNK))
-            side_add(q)
-            if nxt < N_PAIRS:
-                x_quant((nxt, 0, 0, CHUNK))
-            finish(q, 0)
-            if nxt < N_PAIRS:
-                x_quant((nxt, 1, 0, CHUNK))
-        store(N_PAIRS - 1, 0, SLICE)
-        finish(N_PAIRS - 1, 1)
-        store(N_PAIRS - 1, SLICE, SLICE)
+                    x_copy((q, g, 0, CHUNK))
+                    x_quant((q, g, 0, CHUNK))
+            else:
+                pair_copy(q)
+                pair_quant(q)
+
+        def w_prepare(i, k):
+            w_copy(i, k)
+            w_quant(k)
+
+        for i, k in enumerate(W_FIRST):
+            w_transposes(i, k)
+        if not SPLIT_TRANSPOSES:
+            for i, k in enumerate(W_LATER):
+                w_transposes(5 + i, k)
+        for i, k in enumerate(W_FIRST):
+            w_prepare(i, k)
+        x_copy(HEAD_UNITS[0])
+        x_quant(HEAD_UNITS[0])
+        passes(0)
+        if SPLIT_TRANSPOSES:
+            for i, k in enumerate(W_LATER):
+                w_transposes(5 + i, k)
+        for i, k in enumerate(W_LATER):
+            w_prepare(5 + i, k)
+        x_copy(HEAD_UNITS[1])
+        x_quant(HEAD_UNITS[1])
+        passes(1)
+        x_copy(HEAD_UNITS[2])
+        x_quant(HEAD_UNITS[2])
+        prepare(1)
+        LAST = N_PAIRS - 1
+        for q in range(N_PAIRS):
+            passes(q + 2)
+            if q >= 1:
+                main_copy(q - 1, 1)
+                side_add(q - 1, 0)
+                side_add(q - 1, 1)
+                store(q - 1, 0, CHUNK)
+            if q == LAST:
+                break
+            if q < EARLY:
+                main_copy(q, 0)
+                prepare(q + 2)
+            else:
+                prepare(q + 2)
+                main_copy(q, 0)
+        side_copy(LAST)
+        side_add(LAST, 1)
+        main_add(LAST, 0)
+        store(LAST, 0, SLICE)
+        main_add(LAST, 1)
+        store(LAST, SLICE, SLICE)

@@ -20,15 +20,15 @@ CHUNK = 512
 N_PAIRS = 8
 LINE = 16
 BASE = 16
-SPLIT_HEAD = 176
+SPLIT_HEAD = 224
 SPLIT = 320
 W_FIRST = (6, 5, 4, 0, 3)
 W_LATER = (2, 1)
 PINNED = True
 HEAD_PAIRS = 3
 FINE_PAIRS = 3
-EARLY = 1
-W_ON_VECTOR = 0
+EARLY = 0
+W_ON_VECTOR = 2
 HEAD_UNITS = [(0, 0, 0, SLICE), (0, 0, SLICE, SLICE), (0, 1, 0, CHUNK)]
 UNITS = [(q, g, 0, CHUNK) for q in range(1, N_PAIRS) for g in range(G)]
 SPLIT_TRANSPOSES = False
@@ -154,14 +154,13 @@ def tile_stackeddirectionalconv3d_t_kernel(tc, x, W, out):
             t = stage.tile([P, G, CHUNK, PACK], BF16, name="grouped2", align_bytes=64)
             grouped[q] = t
             raw = x_raw[q][:]
-            for g in range(G):
-                nc.scalar.copy(
-                    out=runs4(t[:, g, 0:SPLIT, :], "p (c i) t -> p c t i"),
-                    in_=runs4(raw[:, g, :, 0:SPLIT], "p t (c i) -> p c t i"),
-                )
+            nc.scalar.copy(
+                out=runs4(t[:, 1, :, :], "p (c i) t -> p c t i"),
+                in_=runs4(raw[:, 1, :, :], "p t (c i) -> p c t i"),
+            )
             nc.vector.tensor_copy(
-                out=runs4(t[:, :, SPLIT:CHUNK, :], "p g (c i) t -> p g c t i"),
-                in_=runs4(raw[:, :, :, SPLIT:CHUNK], "p g t (c i) -> p g c t i"),
+                out=runs4(t[:, 0, :, :], "p (c i) t -> p c t i"),
+                in_=runs4(raw[:, 0, :, :], "p t (c i) -> p c t i"),
             )
 
         def pair_quant(q):

@@ -20,18 +20,16 @@ CHUNK = 512
 N_PAIRS = 8
 LINE = 16
 BASE = 16
-SPLIT_HEAD = 224
+SPLIT_HEAD = 256
 SPLIT = 320
 W_FIRST = (6, 5, 4, 0, 3)
 W_LATER = (2, 1)
 PINNED = True
 HEAD_PAIRS = 3
 FINE_PAIRS = 3
-EARLY = 0
-W_ON_VECTOR = 2
+W_ON_VECTOR = 0
 HEAD_UNITS = [(0, 0, 0, SLICE), (0, 0, SLICE, SLICE), (0, 1, 0, CHUNK)]
 UNITS = [(q, g, 0, CHUNK) for q in range(1, N_PAIRS) for g in range(G)]
-SPLIT_TRANSPOSES = False
 
 
 def tile_stackeddirectionalconv3d_t_kernel(tc, x, W, out):
@@ -154,13 +152,14 @@ def tile_stackeddirectionalconv3d_t_kernel(tc, x, W, out):
             t = stage.tile([P, G, CHUNK, PACK], BF16, name="grouped2", align_bytes=64)
             grouped[q] = t
             raw = x_raw[q][:]
-            nc.scalar.copy(
-                out=runs4(t[:, 1, :, :], "p (c i) t -> p c t i"),
-                in_=runs4(raw[:, 1, :, :], "p t (c i) -> p c t i"),
-            )
+            for g in range(G):
+                nc.scalar.copy(
+                    out=runs4(t[:, g, 0:SPLIT, :], "p (c i) t -> p c t i"),
+                    in_=runs4(raw[:, g, :, 0:SPLIT], "p t (c i) -> p c t i"),
+                )
             nc.vector.tensor_copy(
-                out=runs4(t[:, 0, :, :], "p (c i) t -> p c t i"),
-                in_=runs4(raw[:, 0, :, :], "p t (c i) -> p c t i"),
+                out=runs4(t[:, :, SPLIT:CHUNK, :], "p g (c i) t -> p g c t i"),
+                in_=runs4(raw[:, :, :, SPLIT:CHUNK], "p g t (c i) -> p g c t i"),
             )
 
         def pair_quant(q):
@@ -286,25 +285,23 @@ def tile_stackeddirectionalconv3d_t_kernel(tc, x, W, out):
 
         for i, k in enumerate(W_FIRST):
             w_transposes(i, k)
-        if not SPLIT_TRANSPOSES:
-            for i, k in enumerate(W_LATER):
-                w_transposes(5 + i, k)
+        for i, k in enumerate(W_LATER):
+            w_transposes(5 + i, k)
         for i, k in enumerate(W_FIRST):
             w_prepare(i, k)
-        x_copy(HEAD_UNITS[0])
-        x_quant(HEAD_UNITS[0])
+        early = HEAD_UNITS + [(q, g, 0, CHUNK) for q in range(1, FINE_PAIRS) for g in range(G)]
+        x_copy(early[0])
+        x_quant(early[0])
         passes(0)
-        if SPLIT_TRANSPOSES:
-            for i, k in enumerate(W_LATER):
-                w_transposes(5 + i, k)
+        x_copy(early[1])
         for i, k in enumerate(W_LATER):
             w_prepare(5 + i, k)
-        x_copy(HEAD_UNITS[1])
-        x_quant(HEAD_UNITS[1])
-        passes(1)
-        x_copy(HEAD_UNITS[2])
-        x_quant(HEAD_UNITS[2])
-        prepare(1)
+        for j in range(1, len(early)):
+            if j + 1 < len(early):
+                x_copy(early[j + 1])
+            x_quant(early[j])
+            if j == 1:
+                passes(1)
         LAST = N_PAIRS - 1
         for q in range(N_PAIRS):
             passes(q + 2)
@@ -315,12 +312,9 @@ def tile_stackeddirectionalconv3d_t_kernel(tc, x, W, out):
                 store(q - 1, 0, CHUNK)
             if q == LAST:
                 break
-            if q < EARLY:
-                main_copy(q, 0)
+            if q + 2 >= FINE_PAIRS:
                 prepare(q + 2)
-            else:
-                prepare(q + 2)
-                main_copy(q, 0)
+            main_copy(q, 0)
         side_copy(LAST)
         side_add(LAST, 1)
         main_add(LAST, 0)

from contextlib import ExitStack

import concourse.mybir as mybir
from concourse.masks import make_identity

FLOPS = 2 * 4096 * 1024 * 896

F32 = mybir.dt.float32
BF16 = mybir.dt.bfloat16
U32 = mybir.dt.uint32
U8 = mybir.dt.uint8
FP8X4 = mybir.dt.float8_e4m3fn_x4
ADD = mybir.AluOpType.add

P = 128
PACK = 4
G = 2
SLICE = 256
CHUNK = 512
N_PAIRS = 8
LINE = 16
BASE = 16
SPLIT_HEAD = 256
SPLIT = 320
W_FIRST = (6, 5, 4, 0, 3)
W_LATER = (2, 1)
PINNED = True
HEAD_PAIRS = 3
FINE_PAIRS = 3
W_ON_VECTOR = 0
HEAD_UNITS = [(0, 0, 0, SLICE), (0, 0, SLICE, SLICE), (0, 1, 0, CHUNK)]
UNITS = [(q, g, 0, CHUNK) for q in range(1, N_PAIRS) for g in range(G)]


def tile_stackeddirectionalconv3d_t_kernel(tc, x, W, out):
    nc = tc.nc
    with ExitStack() as ctx:
        if PINNED:
            ctx.enter_context(tc.manual_schedule())
        keep = ctx.enter_context(tc.tile_pool(name="keep", bufs=1))
        stage = ctx.enter_context(tc.tile_pool(name="stage", bufs=3))
        psum = ctx.enter_context(tc.psum_pool(name="psum", bufs=1))

        x_codes = keep.tile([P, N_PAIRS, G, CHUNK], U32, name="x_codes", align_bytes=64)
        x_scales = keep.tile([P, N_PAIRS, G, CHUNK], U8, name="x_scales", align_bytes=64)
        w_codes = keep.tile([P, 7, G * P], U32, name="w_codes", align_bytes=64)
        w_scales = keep.tile([P, 7, G * P], U8, name="w_scales", align_bytes=64)
        zero_bf = keep.tile([P, P * PACK], BF16, name="zero_bf", align_bytes=64)
        zero_codes = keep.tile([P, P], U32, name="zero_codes", align_bytes=64)
        zero_scales = keep.tile([P, P], U8, name="zero_scales", align_bytes=64)
        ident = keep.tile([P, P], F32, name="ident")
        res = keep.tile([P, N_PAIRS, CHUNK], F32, name="res")

        w_raw = {}

        def load_w(k):
            w_raw[k] = keep.tile([P, 1024], BF16, name="w_raw%d" % k)
            nc.sync.dma_start(out=w_raw[k][:], in_=W[P * k : P * (k + 1), :])

        x_raw = {}

        def load_x(unit):
            q, g, c0, n = unit
            if q < FINE_PAIRS:
                x_raw[unit] = keep.tile([P, PACK, n], BF16, name="x_raw_%d_%d_%d" % (q, g, c0))[:]
            else:
                if g == 0:
                    x_raw[q] = keep.tile([P, G, PACK, CHUNK], BF16, name="x_raw_%d" % q)
                x_raw[unit] = x_raw[q][:, g, :, :]
            b, qq = divmod(q, 4)
            xb = x[b].rearrange("k t r c -> k (t r c)")
            for u in range(2):
                lo = 512 * g + 256 * u
                rows = xb[lo : lo + 256, CHUNK * qq + c0 : CHUNK * qq + c0 + n]
                nc.sync.dma_start(
                    out=x_raw[unit][:, 2 * u : 2 * u + 2, :],
                    in_=rows.rearrange("(p e) w -> p e w", e=2),
                )

        for k in W_FIRST:
            load_w(k)
        load_x(HEAD_UNITS[0])
        for k in W_LATER:
            load_w(k)
        for unit in HEAD_UNITS[1:] + UNITS:
            load_x(unit)

        def lines(ap):
            return ap.rearrange("p (l c) -> p l c", c=LINE)

        make_identity(nc, ident[:])
        nc.vector.memset(zero_bf[:], 0.0)
        nc.vector.memset(lines(res[:, N_PAIRS - 1, :])[:, :, LINE - 1 : LINE], 0.0)
        nc.vector.quantize_mx(out=zero_codes[:].bitcast(FP8X4), scales=zero_scales[:], in_=zero_bf[:])

        def bank(i, name):
            return psum.tile([P, 512], F32, name=name, tag="bank%d" % i)

        wt = {}

        def w_transposes(i, k):
            words = w_raw[k][:].bitcast(F32)
            wt[k] = bank(i, "wt%d" % k)
            for j in range(4):
                nc.tensor.transpose(wt[k][:, P * j : P * (j + 1)], words[:, P * j : P * (j + 1)], ident[:])

        w_grouped = {}

        def w_copy(i, k):
            w_grouped[k] = stage.tile([P, G * P * PACK], BF16, name="w_grouped", align_bytes=64)
            dst = w_grouped[k][:].bitcast(F32).rearrange("p (g o u) -> p g o u", g=G, u=2)
            src = wt[k][:].rearrange("p (g u o) -> p g o u", g=G, u=2)
            if W_ON_VECTOR and i % W_ON_VECTOR == W_ON_VECTOR - 1:
                nc.vector.tensor_copy(out=dst, in_=src)
            else:
                nc.scalar.copy(out=dst, in_=src)

        def w_quant(k):
            nc.vector.quantize_mx(
                out=w_codes[:, k, :].bitcast(FP8X4), scales=w_scales[:, k, :], in_=w_grouped[k][:]
            )

        grouped = {}

        def runs4(ap, order):
            return ap.rearrange(order, i=4)

        def x_copy(unit):
            q, g, c0, n = unit
            split = (SPLIT_HEAD if q < HEAD_PAIRS else SPLIT) * n // CHUNK
            t = stage.tile([P, CHUNK, PACK], BF16, name="grouped", align_bytes=64)
            grouped[unit] = t
            raw = x_raw[unit]
            nc.scalar.copy(
                out=runs4(t[:, 0:split, :], "p (c i) t -> p c t i"),
                in_=runs4(raw[:, :, 0:split], "p t (c i) -> p c t i"),
            )
            nc.vector.tensor_copy(
                out=runs4(t[:, split:n, :], "p (c i) t -> p c t i"),
                in_=runs4(raw[:, :, split:n], "p t (c i) -> p c t i"),
            )

        def x_quant(unit):
            q, g, c0, n = unit
            nc.vector.quantize_mx(
                out=x_codes[:, q, g, c0 : c0 + n].bitcast(FP8X4),
                scales=x_scales[:, q, g, c0 : c0 + n],
                in_=grouped[unit][:, 0:n, :].rearrange("p w j -> p (w j)"),
            )

        def pair_copy(q):
            t = stage.tile([P, G, CHUNK, PACK], BF16, name="grouped2", align_bytes=64)
            grouped[q] = t
            raw = x_raw[q][:]
            for g in range(G):
                nc.scalar.copy(
                    out=runs4(t[:, g, 0:SPLIT, :], "p (c i) t -> p c t i"),
                    in_=runs4(raw[:, g, :, 0:SPLIT], "p t (c i) -> p c t i"),
                )
            nc.vector.tensor_copy(
                out=runs4(t[:, :, SPLIT:CHUNK, :], "p g (c i) t -> p g c t i"),
                in_=runs4(raw[:, :, :, SPLIT:CHUNK], "p g t (c i) -> p g c t i"),
            )

        def pair_quant(q):
            nc.vector.quantize_mx(
                out=x_codes[:, q, :, :].rearrange("p g c -> p (g c)").bitcast(FP8X4),
                scales=x_scales[:, q, :, :].rearrange("p g c -> p (g c)"),
                in_=grouped[q][:].rearrange("p g w j -> p (g w j)"),
            )

        SHIFT = {4: (-LINE, 0), 0: (0, 0), 3: (LINE, 0), 1: (0, -1), 2: (0, 1)}

        def side(q, g, c0=0, n=CHUNK):
            return [((q, 0), c0, n, 6, g, (q, c0)), ((q, 1), c0, n, 5, g, (q, c0))]

        def centre(q, h, g, ks):
            s = 2 * q + h
            found = []
            for k in ks:
                shift, d = SHIFT[k]
                if not 0 <= s % 8 + d <= 7:
                    continue
                found.append(((q, 2 + h), BASE + shift, SLICE, k, g, ((s + d) // 2, SLICE * ((s + d) % 2))))
                if k == 4 and g == 0:
                    found.append(((q, 2 + h), SLICE, P, k, g, None))
            return found

        plan = []
        for q in range(N_PAIRS):
            seg = []
            if q == 0:
                plan.append(side(q, 0, 0, SLICE) + centre(q, 0, 0, (4, 0, 3)))
                plan.append(side(q, 0, SLICE, SLICE) + centre(q, 1, 0, (4, 0, 3, 1)) + centre(q, 0, 0, (2,)))
                seg += side(q, 1) + centre(q, 0, 1, (4, 0, 3, 2)) + centre(q, 1, 1, (4, 0, 3, 1))
            elif q == 1:
                for g in range(G):
                    seg += centre(q - 1, 1, g, (2,)) + side(q, g)
                    seg += centre(q, 0, g, (4, 0, 3, 1, 2)) + centre(q, 1, g, (4, 0, 3, 1))
            else:
                for g in range(G):
                    seg += centre(q - 1, 1, g, (2,))
                for g in range(G):
                    seg += side(q, g)
                for h in range(2):
                    for k in (4, 0, 3, 1, 2) if h == 0 else (4, 0, 3, 1):
                        for g in range(G):
                            seg += centre(q, h, g, (k,))
            plan.append(seg)
        flat = [item[0] for seg in plan for item in seg]
        first = {}
        last = {}
        for i, key in enumerate(flat):
            if key not in first:
                first[key] = i
            last[key] = i
        banks = {}
        count = [0]

        def passes(part):
            for key, lo, n, k, g, xat in plan[part]:
                if key not in banks:
                    banks[key] = bank(4 * (key[0] % 2) + key[1], "acc%d" % key[1])
                if xat is None:
                    rhs, rhs_scale = zero_codes[:], zero_scales[:]
                else:
                    rhs = x_codes[:, xat[0], g, xat[1] : xat[1] + n]
                    rhs_scale = x_scales[:, xat[0], g, xat[1] : xat[1] + n]
                i = count[0]
                count[0] = i + 1
                nc.tensor.matmul_mx(
                    out=banks[key][:, lo : lo + n],
                    lhsT=w_codes[:, k, P * g : P * (g + 1)].bitcast(FP8X4),
                    lhsT_scale=w_scales[:, k, P * g : P * (g + 1)],
                    rhs=rhs.bitcast(FP8X4),
                    rhs_scale=rhs_scale,
                    start=(first[key] == i),
                    stop=(last[key] == i),
                )

        def main_copy(q, h):
            nc.scalar.copy(
                out=res[:, q, SLICE * h : SLICE * (h + 1)], in_=banks[(q, 2 + h)][:, BASE : BASE + SLICE]
            )

        def main_add(q, h):
            cols = slice(SLICE * h, SLICE * (h + 1))
            nc.vector.tensor_tensor(
                out=res[:, q, cols], in0=res[:, q, cols], in1=banks[(q, 2 + h)][:, BASE : BASE + SLICE], op=ADD
            )

        def side_copy(q):
            nc.scalar.copy(
                out=lines(res[:, q, :])[:, :, 0 : LINE - 1], in_=lines(banks[(q, 0)][:])[:, :, 1:LINE]
            )

        def side_add(q, which):
            r3 = lines(res[:, q, :])
            y3 = lines(banks[(q, which)][:])
            if which == 1:
                dst, src = r3[:, :, 1:LINE], y3[:, :, 0 : LINE - 1]
            else:
                dst, src = r3[:, :, 0 : LINE - 1], y3[:, :, 1:LINE]
            nc.vector.tensor_tensor(out=dst, in0=dst, in1=src, op=ADD)

        def store(q, lo, n):
            b, qq = divmod(q, 4)
            ob = out[b].rearrange("o t r c -> o (t r c)")
            nc.sync.dma_start(out=ob[:, CHUNK * qq + lo : CHUNK * qq + lo + n], in_=res[:, q, lo : lo + n])

        def prepare(q):
            if q >= N_PAIRS:
                return
            if q < FINE_PAIRS:
                for g in range(G):
                    x_copy((q, g, 0, CHUNK))
                    x_quant((q, g, 0, CHUNK))
            else:
                pair_copy(q)
                pair_quant(q)

        def w_prepare(i, k):
            w_copy(i, k)
            w_quant(k)

        for i, k in enumerate(W_FIRST):
            w_transposes(i, k)
        for i, k in enumerate(W_LATER):
            w_transposes(5 + i, k)
        for i, k in enumerate(W_FIRST):
            w_prepare(i, k)
        early = HEAD_UNITS + [(q, g, 0, CHUNK) for q in range(1, FINE_PAIRS) for g in range(G)]
        x_copy(early[0])
        x_quant(early[0])
        passes(0)
        x_copy(early[1])
        for i, k in enumerate(W_LATER):
            w_prepare(5 + i, k)
        for j in range(1, len(early)):
            if j + 1 < len(early):
                x_copy(early[j + 1])
            x_quant(early[j])
            if j == 1:
                passes(1)
        LAST = N_PAIRS - 1
        for q in range(N_PAIRS):
            passes(q + 2)
            if q >= 1:
                main_copy(q - 1, 1)
                side_add(q - 1, 0)
                side_add(q - 1, 1)
                store(q - 1, 0, CHUNK)
            if q == LAST:
                break
            if q + 2 >= FINE_PAIRS:
                prepare(q + 2)
            main_copy(q, 0)
        side_copy(LAST)
        side_add(LAST, 1)
        main_add(LAST, 0)
        store(LAST, 0, SLICE)
        main_add(LAST, 1)
        store(LAST, SLICE, SLICE)
